import numpy as np
import ml_dtypes


def mxq(x, axis, fmt="e4m3"):
    dtype, down = {"e4m3": (ml_dtypes.float8_e4m3fn, 7), "e5m2": (ml_dtypes.float8_e5m2, 14)}[fmt]
    v = np.moveaxis(np.asarray(x, np.float32).astype(ml_dtypes.bfloat16).astype(np.float64), axis, -1)
    blocks = v.reshape(v.shape[:-1] + (-1, 32))
    amax = np.abs(blocks).max(-1, keepdims=True)
    byte = np.maximum(np.where(amax > 0, np.frexp(amax)[1] - 1 + 127, 0) - down, 1)
    scale = np.exp2(byte - 127.0)
    codes = (blocks / scale).astype(np.float32).astype(dtype).astype(np.float64)
    return np.moveaxis((codes * scale).reshape(v.shape), -1, axis)


WIDE = False


def mx_kscale(k):
    if not WIDE:
        return np.ones(k)
    levels = np.array([10, -10, 5, -5, 0])
    a = np.random.permutation(np.resize(levels, k // 512 * 4)).reshape(k // 512, 4)
    idx = np.arange(k)
    return np.exp2(a[idx // 512, idx % 128 // 32])


BF16 = ml_dtypes.bfloat16


def bf(x):
    return np.asarray(x, np.float32).astype(BF16)


def f64(x):
    return np.asarray(x).astype(np.float64)


E2M1 = np.array([0.0, 0.5, 1.0, 1.5, 2.0, 3.0, 4.0, 6.0, -0.0, -0.5, -1.0, -1.5, -2.0, -3.0, -4.0, -6.0])


def pack_weight(w, fmt):
    k, n = w.shape
    w = f64(bf(w)).reshape(k // 32, 32, n)
    amax = np.abs(w).max(1)
    if fmt == "e4m3":
        byte = np.frexp(amax)[1] - 1 + 127 - 7
    else:
        mant, ex = np.frexp(amax / 6.0)
        byte = np.where(mant > 0.5, ex, ex - 1) + 127
    byte = np.clip(np.where(amax > 0, byte, 1), 1, 254)
    scaled = (w * np.exp2(127.0 - byte)[:, None, :]).reshape(k, n).astype(np.float32)
    by_word = np.ascontiguousarray(scaled.reshape(k // 512, 128, 4, n).transpose(0, 1, 3, 2))
    if fmt == "e4m3":
        words = by_word.astype(ml_dtypes.float8_e4m3fn).view(np.uint8)
    else:
        c = by_word.astype(ml_dtypes.float4_e2m1fn).view(np.uint8) & 0xF
        words = c[..., 0::2] | (c[..., 1::2] << 4)
    return np.ascontiguousarray(words), np.ascontiguousarray(byte.astype(np.uint8).reshape(k // 512, 16, n))


def unpack_weight(words, scales, fmt):
    g, p, n, _ = words.shape
    if fmt == "e4m3":
        vals = np.ascontiguousarray(words).view(ml_dtypes.float8_e4m3fn).astype(np.float64)
    else:
        nib = np.empty((g, p, n, 4), np.uint8)
        nib[..., 0::2] = words & 0xF
        nib[..., 1::2] = words >> 4
        vals = E2M1[nib]
    vals = vals * np.repeat(np.exp2(scales.astype(np.float64) - 127.0), 8, axis=1)[..., None]
    return vals.transpose(0, 1, 3, 2).reshape(g * 512, n)


B, STACK, TUBE, CH, IMG, PATCH, EMBED = 4, 16, 2, 1, 96, 16, 1024
GH = IMG // PATCH
GW = IMG // PATCH
GD = STACK // TUBE
K = TUBE * CH * PATCH * PATCH


def _sincos_1d(dim, pos):
    omega = 1.0 / (10000.0 ** (np.arange(dim // 2, dtype=np.float64) / (dim / 2.0)))
    out = pos[:, None].astype(np.float64) * omega[None, :]
    return np.concatenate([np.sin(out), np.cos(out)], axis=1)


def get_3d_sincos_pos_embed(grid_h, grid_w, grid_depth, embed_dim):
    dim_t = embed_dim // 4
    dim_s = embed_dim - dim_t
    emb_t = _sincos_1d(dim_t, np.arange(grid_depth))
    emb_h = _sincos_1d(dim_s // 2, np.arange(grid_h))
    emb_w = _sincos_1d(dim_s - dim_s // 2, np.arange(grid_w))
    emb_hw = np.concatenate([np.repeat(emb_h, grid_w, axis=0), np.tile(emb_w, (grid_h, 1))], axis=1)
    ns = grid_h * grid_w
    return np.concatenate([np.repeat(emb_t, ns, axis=0), np.tile(emb_hw, (grid_depth, 1))], axis=1)


def setup_inputs():
    s = mx_kscale(K)
    sv = s.reshape(TUBE, CH, PATCH, PATCH)[:, :, None, :, None, :]
    video = np.random.standard_normal((B, GD, TUBE, CH, GH, PATCH, GW, PATCH)) * sv
    w_nk = np.random.standard_normal((EMBED, K)) / np.sqrt(K) / s[None, :]
    words, scales = pack_weight(np.ascontiguousarray(w_nk.T), "e4m3")
    return {"video": bf(video.reshape(B, STACK, CH, IMG, IMG)),
            "W_words": words,
            "W_scales": scales,
            "b": bf(np.random.standard_normal(EMBED) * 0.3),
            "pos_embed": bf(get_3d_sincos_pos_embed(GH, GW, GD, EMBED)[None])}


def reference(video, W_words, W_scales, b, pos_embed):
    video = f64(video)
    B_, T, C, H, W_ = video.shape
    p = PATCH
    gh, gw = H // p, W_ // p
    ns = gh * gw
    x = video.reshape(B_ * T, C, gh, p, gw, p)
    x = x.transpose(0, 2, 4, 1, 3, 5)
    x = x.reshape(B_, T, ns, C * p * p)
    x = x.reshape(B_, GD, TUBE, ns, C * p * p)
    x = x.transpose(0, 1, 3, 2, 4)
    tubelets = x.reshape(B_, GD * ns, TUBE * C * p * p)
    tokens = (mxq(tubelets, 2, "e4m3") @ unpack_weight(W_words, W_scales, "e4m3")) + f64(b) + f64(pos_embed)
    return tokens

@@ -1,0 +1,212 @@
+from contextlib import ExitStack
+
+import concourse.mybir as mybir
+from concourse.masks import make_identity
+
+F32 = mybir.dt.float32
+BF16 = mybir.dt.bfloat16
+I32 = mybir.dt.int32
+U32 = mybir.dt.uint32
+U8 = mybir.dt.uint8
+FP8X4 = mybir.dt.float8_e4m3fn_x4
+ADD = mybir.AluOpType.add
+
+P = 128
+BATCH = 4
+TUBES = 8
+TUBE = 2
+GRID = 6
+PATCH = 16
+EMBED = 1024
+K = TUBE * PATCH * PATCH
+BANDS = BATCH * TUBES * 2
+BAND_GRID_ROWS = GRID // 2
+BAND_ROWS = BAND_GRID_ROWS * GRID
+STRIP = PATCH * GRID * PATCH
+N_HALF = 512
+MAIN_ROWS = 8
+TOKENS = BATCH * TUBES * GRID * GRID
+POOL_EVERY = 3
+FLOPS = 2 * TOKENS * K * EMBED
+
+
+def tile_tubeletembedding_kernel(tc, video, W_words, W_scales, b, pos_embed, out):
+    nc = tc.nc
+    with ExitStack() as ctx:
+        keep = ctx.enter_context(tc.tile_pool(name="keep", bufs=1))
+        results = ctx.enter_context(tc.tile_pool(name="results", bufs=4))
+        psum_flip = ctx.enter_context(tc.psum_pool(name="psum_flip", bufs=3))
+        psum_acc = ctx.enter_context(tc.psum_pool(name="psum_acc", bufs=3))
+        psum_bias = ctx.enter_context(tc.psum_pool(name="psum_bias", bufs=1))
+
+        strips = video[:, :, 0, :, :].rearrange(
+            "b (d ts) (half il py) w -> (b d) ts half il (py w)",
+            ts=TUBE, half=2, il=BAND_GRID_ROWS, py=PATCH,
+        )
+        pos_bands = pos_embed[0].rearrange("(q r) n -> q r n", r=BAND_ROWS)
+        out_bands = out.rearrange("b (q r) n -> (b q) r n", r=BAND_ROWS)
+
+        bias_row = keep.tile([P, EMBED], BF16, name="bias_row")
+        nc.vector.memset(bias_row[:], 0.0)
+        ones = keep.tile([P, P], BF16, name="ones")
+        nc.vector.memset(ones[:], 1.0)
+        w_scales = keep.tile([P, EMBED], U8, name="w_scales", align_bytes=64)
+        nc.vector.memset(w_scales[:].bitcast(I32), 0)
+        pixels = [keep.tile([P, TUBE, STRIP], BF16, name="pixels%d" % t) for t in range(2)]
+        nc.vector.memset(pixels[1][:].bitcast(I32), 0)
+        identity = keep.tile([P, P], F32, name="identity")
+        make_identity(nc, identity[:])
+
+        nc.scalar.dma_start(out=bias_row[0:1, :], in_=b.rearrange("(o n) -> o n", o=1))
+        pos_bf = keep.tile([P, 3, EMBED], BF16, name="pos_bf")
+
+        def load_pos_main(y):
+            nc.sync.dma_start(
+                out=pos_bf[:, y, :], in_=pos_bands[:, MAIN_ROWS * y : MAIN_ROWS * (y + 1), :]
+            )
+
+        def load_pixels(t, lanes):
+            for ts in range(TUBE):
+                for lane in range(lanes):
+                    nc.sync.dma_start(
+                        out=pixels[t][lane:P:2, ts, :], in_=strips[:, ts, :, 2 * t + lane, :]
+                    )
+
+        load_pixels(0, 2)
+        load_pos_main(0)
+        for quadrant in range(4):
+            nc.sync.dma_start(
+                out=w_scales[32 * quadrant : 32 * quadrant + 4, :].bitcast(I32),
+                in_=W_scales[0, 4 * quadrant : 4 * quadrant + 4, :].bitcast(I32),
+            )
+        w_codes = keep.tile([P, 4 * EMBED], U8, name="w_codes", align_bytes=64)
+        nc.sync.dma_start(
+            out=w_codes[:].bitcast(I32),
+            in_=W_words[0].rearrange("p n t -> p (n t)").bitcast(I32),
+        )
+        load_pixels(1, 1)
+        load_pos_main(1)
+        for batch in range(BATCH):
+            nc.sync.dma_start(
+                out=pos_bf[32 * batch : 32 * (batch + 1), 2, :],
+                in_=pos_bands[:, 2 * MAIN_ROWS : BAND_ROWS, :],
+            )
+
+        bias_psum = psum_bias.tile([P, 2, N_HALF], F32, name="bias_psum")
+        bias_all = keep.tile([P, EMBED], F32, name="bias_all")
+        for h in range(2):
+            cols = slice(N_HALF * h, N_HALF * (h + 1))
+            nc.tensor.matmul(
+                out=bias_psum[:, h, :], lhsT=ones[:], rhs=bias_row[:, cols], start=True, stop=True
+            )
+            nc.scalar.copy(out=bias_all[:, cols], in_=bias_psum[:, h, :])
+        addend = keep.tile([P, 3, EMBED], F32, name="addend")
+
+        def make_addend(kind):
+            for h in range(2):
+                cols = slice(N_HALF * h, N_HALF * (h + 1))
+                nc.gpsimd.tensor_tensor(
+                    out=addend[:, kind, cols], in0=pos_bf[:, kind, cols], in1=bias_all[:, cols],
+                    op=ADD,
+                )
+
+        sorted_words = [
+            keep.tile([P, GRID, 2, P], F32, name="sorted_words%d" % t) for t in range(2)
+        ]
+        grouped_main = keep.tile([P, 2, BANDS, 4, 8], BF16, name="grouped_main", align_bytes=64)
+        grouped_last = keep.tile([P, BANDS, 8], BF16, name="grouped_last", align_bytes=64)
+        x_codes = keep.tile([P, TOKENS], U32, name="x_codes", align_bytes=64)
+        x_scales = keep.tile([P, TOKENS], U8, name="x_scales", align_bytes=64)
+
+        def sort_words(copy, t):
+            for ts in range(TUBE):
+                half = slice(ts * (P // 2), (ts + 1) * (P // 2))
+                by_column = pixels[t][:, ts, :].bitcast(F32).rearrange(
+                    "p (py j q u) -> p j u py q", py=PATCH, j=GRID, q=4, u=2
+                )
+                for jp in range(GRID // 2):
+                    pair = slice(2 * jp, 2 * jp + 2)
+                    copy(
+                        out=sorted_words[t][:, pair, :, half].rearrange(
+                            "p j u (py q) -> p j u py q", q=4
+                        ),
+                        in_=by_column[:, pair],
+                    )
+
+        def flip(t, jp):
+            flipped = psum_flip.tile([P, 2, 2, P], F32, name="flipped")
+            for jj in range(2):
+                for u in range(2):
+                    nc.tensor.transpose(
+                        flipped[:, jj, u, :], sorted_words[t][:, 2 * jp + jj, u, :], identity[:]
+                    )
+            return flipped
+
+        def gather_row_pair(rp, flipped):
+            il = rp // 3
+            source = flipped[:, :, :, il % 2 : P : 2].rearrange("p jj u q -> p q jj u")
+            if rp < 8:
+                target = grouped_main[:].bitcast(F32)[:, rp // 4, :, rp % 4, :]
+            else:
+                target = grouped_last[:].bitcast(F32)
+            nc.scalar.copy(out=target.rearrange("p q (jj u) -> p q jj u", u=2), in_=source)
+
+        def embed(tile_index, grouped, kind, rows):
+            tokens = slice(P * tile_index, P * (tile_index + 1))
+            nc.vector.quantize_mx(
+                out=x_codes[:, tokens].bitcast(FP8X4), scales=x_scales[:, tokens], in_=grouped
+            )
+            result = results.tile([P, EMBED], F32, name="result")
+            for h in range(2):
+                cols = slice(N_HALF * h, N_HALF * (h + 1))
+                acc = psum_acc.tile([P, N_HALF], F32, name="acc")
+                nc.tensor.matmul_mx(
+                    out=acc[:],
+                    lhsT=x_codes[:, tokens].bitcast(FP8X4),
+                    lhsT_scale=x_scales[:, tokens],
+                    rhs=w_codes[:, 4 * N_HALF * h : 4 * N_HALF * (h + 1)].bitcast(FP8X4),
+                    rhs_scale=w_scales[:, cols],
+                    start=True,
+                    stop=True,
+                )
+                if h == 1 and tile_index % POOL_EVERY == 1:
+                    nc.scalar.copy(out=result[:, cols], in_=acc[:])
+                    nc.gpsimd.tensor_tensor(
+                        out=result[:, cols], in0=result[:, cols], in1=addend[:, kind, cols], op=ADD
+                    )
+                else:
+                    nc.vector.tensor_tensor(
+                        out=result[:, cols], in0=acc[:], in1=addend[:, kind, cols], op=ADD
+                    )
+            nc.sync.dma_start(out=rows, in_=result[:])
+
+        def embed_main(y):
+            for batch in range(BATCH):
+                bands = slice(16 * batch, 16 * (batch + 1))
+                embed(
+                    4 * y + batch,
+                    grouped_main[:, y, bands].rearrange("p q a v -> p (q a v)"),
+                    y,
+                    out_bands[bands, MAIN_ROWS * y : MAIN_ROWS * (y + 1), :],
+                )
+
+        make_addend(0)
+        sort_words(nc.vector.tensor_copy, 0)
+        flipped0 = [flip(0, jp) for jp in range(3)]
+        for rp in range(0, 4):
+            gather_row_pair(rp, flipped0[rp % 3])
+        make_addend(1)
+        embed_main(0)
+        for rp in range(4, 6):
+            gather_row_pair(rp, flipped0[rp % 3])
+        sort_words(nc.scalar.copy, 1)
+        for rp in range(6, 9):
+            gather_row_pair(rp, flip(1, rp % 3))
+        make_addend(2)
+        embed_main(1)
+        embed(
+            8,
+            grouped_last[:].rearrange("p q v -> p (q v)"),
+            2,
+            out_bands[:, 2 * MAIN_ROWS : BAND_ROWS, :],
+        )

@@ -20,13 +20,14 @@ PATCH = 16
 EMBED = 1024
 K = TUBE * PATCH * PATCH
 BANDS = BATCH * TUBES * 2
+BATCH_BANDS = BANDS // BATCH
 BAND_GRID_ROWS = GRID // 2
 BAND_ROWS = BAND_GRID_ROWS * GRID
 STRIP = PATCH * GRID * PATCH
 N_HALF = 512
 MAIN_ROWS = 8
 TOKENS = BATCH * TUBES * GRID * GRID
-POOL_EVERY = 3
+BIAS_ROW = 32
 FLOPS = 2 * TOKENS * K * EMBED
 
 
@@ -34,10 +35,9 @@ def tile_tubeletembedding_kernel(tc, video, W_words, W_scales, b, pos_embed, out
     nc = tc.nc
     with ExitStack() as ctx:
         keep = ctx.enter_context(tc.tile_pool(name="keep", bufs=1))
-        results = ctx.enter_context(tc.tile_pool(name="results", bufs=4))
+        results = ctx.enter_context(tc.tile_pool(name="results", bufs=TOKENS // P))
         psum_flip = ctx.enter_context(tc.psum_pool(name="psum_flip", bufs=3))
-        psum_acc = ctx.enter_context(tc.psum_pool(name="psum_acc", bufs=3))
-        psum_bias = ctx.enter_context(tc.psum_pool(name="psum_bias", bufs=1))
+        psum_acc = ctx.enter_context(tc.psum_pool(name="psum_acc", bufs=5))
 
         strips = video[:, :, 0, :, :].rearrange(
             "b (d ts) (half il py) w -> (b d) ts half il (py w)",
@@ -46,24 +46,32 @@ def tile_tubeletembedding_kernel(tc, video, W_words, W_scales, b, pos_embed, out
         pos_bands = pos_embed[0].rearrange("(q r) n -> q r n", r=BAND_ROWS)
         out_bands = out.rearrange("b (q r) n -> (b q) r n", r=BAND_ROWS)
 
-        bias_row = keep.tile([P, EMBED], BF16, name="bias_row")
-        nc.vector.memset(bias_row[:], 0.0)
-        ones = keep.tile([P, P], BF16, name="ones")
-        nc.vector.memset(ones[:], 1.0)
+        def main_rows(y):
+            return slice(2 + MAIN_ROWS * y, 2 + MAIN_ROWS * (y + 1))
+
+        def half_cols(h):
+            return slice(N_HALF * h, N_HALF * (h + 1))
+
+        small_rows = keep.tile([P, EMBED], BF16, name="small_rows")
+        nc.vector.memset(small_rows[:], 0.0)
         w_scales = keep.tile([P, EMBED], U8, name="w_scales", align_bytes=64)
         nc.vector.memset(w_scales[:].bitcast(I32), 0)
-        pixels = [keep.tile([P, TUBE, STRIP], BF16, name="pixels%d" % t) for t in range(2)]
-        nc.vector.memset(pixels[1][:].bitcast(I32), 0)
         identity = keep.tile([P, P], F32, name="identity")
         make_identity(nc, identity[:])
+        pickers = keep.tile([P, 2, P], BF16, name="pickers")
+        nc.vector.memset(pickers[:], 0.0)
+        nc.vector.memset(pickers[BIAS_ROW : BIAS_ROW + 1, :, :], 1.0)
+        nc.vector.tensor_copy(
+            out=pickers[0:32, 0, :].rearrange("k (c m) -> k c m", m=32),
+            in_=identity[0:32, 0:32].unsqueeze(1).to_broadcast([32, BATCH, 32]),
+        )
+        pixels = [keep.tile([P, TUBE, STRIP], BF16, name="pixels%d" % t) for t in range(2)]
+        nc.vector.memset(pixels[1][:].bitcast(I32), 0)
 
-        nc.scalar.dma_start(out=bias_row[0:1, :], in_=b.rearrange("(o n) -> o n", o=1))
-        pos_bf = keep.tile([P, 3, EMBED], BF16, name="pos_bf")
-
-        def load_pos_main(y):
-            nc.sync.dma_start(
-                out=pos_bf[:, y, :], in_=pos_bands[:, MAIN_ROWS * y : MAIN_ROWS * (y + 1), :]
-            )
+        nc.scalar.dma_start(
+            out=small_rows[BIAS_ROW : BIAS_ROW + 1, :], in_=b.rearrange("(o n) -> o n", o=1)
+        )
+        nc.scalar.dma_start(out=small_rows[0:32, :], in_=pos_bands[:, 0:2, :])
 
         def load_pixels(t, lanes):
             for ts in range(TUBE):
@@ -72,49 +80,44 @@ def tile_tubeletembedding_kernel(tc, video, W_words, W_scales, b, pos_embed, out
                         out=pixels[t][lane:P:2, ts, :], in_=strips[:, ts, :, 2 * t + lane, :]
                     )
 
+        pos_bf = keep.tile([P, 2, EMBED], BF16, name="pos_bf")
+        w_codes = keep.tile([P, 4 * EMBED], U8, name="w_codes", align_bytes=64)
         load_pixels(0, 2)
-        load_pos_main(0)
         for quadrant in range(4):
             nc.sync.dma_start(
                 out=w_scales[32 * quadrant : 32 * quadrant + 4, :].bitcast(I32),
                 in_=W_scales[0, 4 * quadrant : 4 * quadrant + 4, :].bitcast(I32),
             )
-        w_codes = keep.tile([P, 4 * EMBED], U8, name="w_codes", align_bytes=64)
         nc.sync.dma_start(
             out=w_codes[:].bitcast(I32),
             in_=W_words[0].rearrange("p n t -> p (n t)").bitcast(I32),
         )
+        nc.sync.dma_start(out=pos_bf[:, 0, :], in_=pos_bands[:, main_rows(0), :])
         load_pixels(1, 1)
-        load_pos_main(1)
-        for batch in range(BATCH):
-            nc.sync.dma_start(
-                out=pos_bf[32 * batch : 32 * (batch + 1), 2, :],
-                in_=pos_bands[:, 2 * MAIN_ROWS : BAND_ROWS, :],
-            )
+        nc.sync.dma_start(out=pos_bf[:, 1, :], in_=pos_bands[:, main_rows(1), :])
 
-        bias_psum = psum_bias.tile([P, 2, N_HALF], F32, name="bias_psum")
-        bias_all = keep.tile([P, EMBED], F32, name="bias_all")
-        for h in range(2):
-            cols = slice(N_HALF * h, N_HALF * (h + 1))
-            nc.tensor.matmul(
-                out=bias_psum[:, h, :], lhsT=ones[:], rhs=bias_row[:, cols], start=True, stop=True
-            )
-            nc.scalar.copy(out=bias_all[:, cols], in_=bias_psum[:, h, :])
         addend = keep.tile([P, 3, EMBED], F32, name="addend")
-
-        def make_addend(kind):
+        bias_all = keep.tile([P, EMBED], F32, name="bias_all")
+        for picker, spread in ((0, addend[:, 0, :]), (1, bias_all[:])):
             for h in range(2):
-                cols = slice(N_HALF * h, N_HALF * (h + 1))
+                acc = psum_acc.tile([P, N_HALF], F32, name="acc")
+                nc.tensor.matmul(
+                    out=acc[:], lhsT=pickers[:, picker, :], rhs=small_rows[:, half_cols(h)],
+                    start=True, stop=True,
+                )
+                nc.scalar.copy(out=spread[:, half_cols(h)], in_=acc[:])
+        for y in range(2):
+            for h in range(2):
                 nc.gpsimd.tensor_tensor(
-                    out=addend[:, kind, cols], in0=pos_bf[:, kind, cols], in1=bias_all[:, cols],
-                    op=ADD,
+                    out=addend[:, 1 + y, half_cols(h)], in0=pos_bf[:, y, half_cols(h)],
+                    in1=bias_all[:, half_cols(h)], op=ADD,
                 )
 
         sorted_words = [
             keep.tile([P, GRID, 2, P], F32, name="sorted_words%d" % t) for t in range(2)
         ]
+        grouped_pair = keep.tile([P, BANDS, 8], BF16, name="grouped_pair", align_bytes=64)
         grouped_main = keep.tile([P, 2, BANDS, 4, 8], BF16, name="grouped_main", align_bytes=64)
-        grouped_last = keep.tile([P, BANDS, 8], BF16, name="grouped_last", align_bytes=64)
         x_codes = keep.tile([P, TOKENS], U32, name="x_codes", align_bytes=64)
         x_scales = keep.tile([P, TOKENS], U8, name="x_scales", align_bytes=64)
 
@@ -142,14 +145,16 @@ def tile_tubeletembedding_kernel(tc, video, W_words, W_scales, b, pos_embed, out
                     )
             return flipped
 
-        def gather_row_pair(rp, flipped):
-            il = rp // 3
-            source = flipped[:, :, :, il % 2 : P : 2].rearrange("p jj u q -> p q jj u")
-            if rp < 8:
-                target = grouped_main[:].bitcast(F32)[:, rp // 4, :, rp % 4, :]
+        def gather_row_pair(il, jp, flipped):
+            rp = BAND_GRID_ROWS * il + jp
+            if rp == 0:
+                target = grouped_pair[:].bitcast(F32)
             else:
-                target = grouped_last[:].bitcast(F32)
-            nc.scalar.copy(out=target.rearrange("p q (jj u) -> p q jj u", u=2), in_=source)
+                target = grouped_main[:].bitcast(F32)[:, (rp - 1) // 4, :, (rp - 1) % 4, :]
+            nc.scalar.copy(
+                out=target.rearrange("p q (jj u) -> p q jj u", u=2),
+                in_=flipped[:, :, :, il % 2 : P : 2].rearrange("p jj u q -> p q jj u"),
+            )
 
         def embed(tile_index, grouped, kind, rows):
             tokens = slice(P * tile_index, P * (tile_index + 1))
@@ -158,7 +163,7 @@ def tile_tubeletembedding_kernel(tc, video, W_words, W_scales, b, pos_embed, out
             )
             result = results.tile([P, EMBED], F32, name="result")
             for h in range(2):
-                cols = slice(N_HALF * h, N_HALF * (h + 1))
+                cols = half_cols(h)
                 acc = psum_acc.tile([P, N_HALF], F32, name="acc")
                 nc.tensor.matmul_mx(
                     out=acc[:],
@@ -169,7 +174,7 @@ def tile_tubeletembedding_kernel(tc, video, W_words, W_scales, b, pos_embed, out
                     start=True,
                     stop=True,
                 )
-                if h == 1 and tile_index % POOL_EVERY == 1:
+                if h == 1 and tile_index % 2 == 1:
                     nc.scalar.copy(out=result[:, cols], in_=acc[:])
                     nc.gpsimd.tensor_tensor(
                         out=result[:, cols], in0=result[:, cols], in1=addend[:, kind, cols], op=ADD
@@ -178,35 +183,27 @@ def tile_tubeletembedding_kernel(tc, video, W_words, W_scales, b, pos_embed, out
                     nc.vector.tensor_tensor(
                         out=result[:, cols], in0=acc[:], in1=addend[:, kind, cols], op=ADD
                     )
-            nc.sync.dma_start(out=rows, in_=result[:])
+                nc.sync.dma_start(out=rows[:, :, cols], in_=result[:, cols])
 
         def embed_main(y):
             for batch in range(BATCH):
-                bands = slice(16 * batch, 16 * (batch + 1))
+                bands = slice(BATCH_BANDS * batch, BATCH_BANDS * (batch + 1))
                 embed(
-                    4 * y + batch,
+                    1 + BATCH * y + batch,
                     grouped_main[:, y, bands].rearrange("p q a v -> p (q a v)"),
-                    y,
-                    out_bands[bands, MAIN_ROWS * y : MAIN_ROWS * (y + 1), :],
+                    1 + y,
+                    out_bands[bands, main_rows(y), :],
                 )
 
-        make_addend(0)
         sort_words(nc.vector.tensor_copy, 0)
-        flipped0 = [flip(0, jp) for jp in range(3)]
-        for rp in range(0, 4):
-            gather_row_pair(rp, flipped0[rp % 3])
-        make_addend(1)
+        for jp in range(GRID // 2):
+            flipped = flip(0, jp)
+            for il in range(2):
+                gather_row_pair(il, jp, flipped)
+            if jp == 0:
+                embed(0, grouped_pair[:].rearrange("p q v -> p (q v)"), 0, out_bands[:, 0:2, :])
         embed_main(0)
-        for rp in range(4, 6):
-            gather_row_pair(rp, flipped0[rp % 3])
         sort_words(nc.scalar.copy, 1)
-        for rp in range(6, 9):
-            gather_row_pair(rp, flip(1, rp % 3))
-        make_addend(2)
+        for jp in range(GRID // 2):
+            gather_row_pair(2, jp, flip(1, jp))
         embed_main(1)
-        embed(
-            8,
-            grouped_last[:].rearrange("p q v -> p (q v)"),
-            2,
-            out_bands[:, 2 * MAIN_ROWS : BAND_ROWS, :],
-        )

@@ -88,29 +88,33 @@ def tile_tubeletembedding_kernel(tc, video, W_words, W_scales, b, pos_embed, out
                 out=w_scales[32 * quadrant : 32 * quadrant + 4, :].bitcast(I32),
                 in_=W_scales[0, 4 * quadrant : 4 * quadrant + 4, :].bitcast(I32),
             )
+        nc.sync.dma_start(out=pos_bf[:, 0, :], in_=pos_bands[:, main_rows(0), :])
         nc.sync.dma_start(
             out=w_codes[:].bitcast(I32),
             in_=W_words[0].rearrange("p n t -> p (n t)").bitcast(I32),
         )
-        nc.sync.dma_start(out=pos_bf[:, 0, :], in_=pos_bands[:, main_rows(0), :])
         load_pixels(1, 1)
         nc.sync.dma_start(out=pos_bf[:, 1, :], in_=pos_bands[:, main_rows(1), :])
 
         addend = keep.tile([P, 3, EMBED], F32, name="addend")
-        bias_all = keep.tile([P, EMBED], F32, name="bias_all")
-        for picker, spread in ((0, addend[:, 0, :]), (1, bias_all[:])):
+
+        def spread_rows(picker, h):
+            acc = psum_acc.tile([P, N_HALF], F32, name="acc")
+            nc.tensor.matmul(
+                out=acc[:], lhsT=pickers[:, picker, :], rhs=small_rows[:, half_cols(h)],
+                start=True, stop=True,
+            )
+            return acc
+
+        for h in range(2):
+            nc.scalar.copy(out=addend[:, 0, half_cols(h)], in_=spread_rows(0, h)[:])
+        bias_all = [spread_rows(1, h) for h in range(2)]
+
+        def make_addend(y):
             for h in range(2):
-                acc = psum_acc.tile([P, N_HALF], F32, name="acc")
-                nc.tensor.matmul(
-                    out=acc[:], lhsT=pickers[:, picker, :], rhs=small_rows[:, half_cols(h)],
-                    start=True, stop=True,
-                )
-                nc.scalar.copy(out=spread[:, half_cols(h)], in_=acc[:])
-        for y in range(2):
-            for h in range(2):
-                nc.gpsimd.tensor_tensor(
-                    out=addend[:, 1 + y, half_cols(h)], in0=pos_bf[:, y, half_cols(h)],
-                    in1=bias_all[:, half_cols(h)], op=ADD,
+                nc.vector.tensor_tensor(
+                    out=addend[:, 1 + y, half_cols(h)], in0=bias_all[h][:],
+                    in1=pos_bf[:, y, half_cols(h)], op=ADD,
                 )
 
         sorted_words = [
@@ -174,15 +178,9 @@ def tile_tubeletembedding_kernel(tc, video, W_words, W_scales, b, pos_embed, out
                     start=True,
                     stop=True,
                 )
-                if h == 1 and tile_index % 2 == 1:
-                    nc.scalar.copy(out=result[:, cols], in_=acc[:])
-                    nc.gpsimd.tensor_tensor(
-                        out=result[:, cols], in0=result[:, cols], in1=addend[:, kind, cols], op=ADD
-                    )
-                else:
-                    nc.vector.tensor_tensor(
-                        out=result[:, cols], in0=acc[:], in1=addend[:, kind, cols], op=ADD
-                    )
+                nc.vector.tensor_tensor(
+                    out=result[:, cols], in0=acc[:], in1=addend[:, kind, cols], op=ADD
+                )
                 nc.sync.dma_start(out=rows[:, :, cols], in_=result[:, cols])
 
         def embed_main(y):
@@ -202,8 +200,10 @@ def tile_tubeletembedding_kernel(tc, video, W_words, W_scales, b, pos_embed, out
                 gather_row_pair(il, jp, flipped)
             if jp == 0:
                 embed(0, grouped_pair[:].rearrange("p q v -> p (q v)"), 0, out_bands[:, 0:2, :])
+                make_addend(0)
         embed_main(0)
         sort_words(nc.scalar.copy, 1)
         for jp in range(GRID // 2):
             gather_row_pair(2, jp, flip(1, jp))
+        make_addend(1)
         embed_main(1)

@@ -38,6 +38,7 @@ def tile_tubeletembedding_kernel(tc, video, W_words, W_scales, b, pos_embed, out
         results = ctx.enter_context(tc.tile_pool(name="results", bufs=TOKENS // P))
         psum_flip = ctx.enter_context(tc.psum_pool(name="psum_flip", bufs=3))
         psum_acc = ctx.enter_context(tc.psum_pool(name="psum_acc", bufs=5))
+        ctx.enter_context(tc.manual_schedule())
 
         strips = video[:, :, 0, :, :].rearrange(
             "b (d ts) (half il py) w -> (b d) ts half il (py w)",
@@ -68,10 +69,13 @@ def tile_tubeletembedding_kernel(tc, video, W_words, W_scales, b, pos_embed, out
         pixels = [keep.tile([P, TUBE, STRIP], BF16, name="pixels%d" % t) for t in range(2)]
         nc.vector.memset(pixels[1][:].bitcast(I32), 0)
 
-        nc.scalar.dma_start(
-            out=small_rows[BIAS_ROW : BIAS_ROW + 1, :], in_=b.rearrange("(o n) -> o n", o=1)
+        nc.gpsimd.dma_start(
+            out=small_rows[BIAS_ROW : BIAS_ROW + 1, :].bitcast(F32),
+            in_=b.rearrange("(o n) -> o n", o=1).bitcast(F32),
         )
-        nc.scalar.dma_start(out=small_rows[0:32, :], in_=pos_bands[:, 0:2, :])
+        nc.gpsimd.dma_start(
+            out=small_rows[0:32, :].bitcast(F32), in_=pos_bands[:, 0:2, :].bitcast(F32)
+        )
 
         def load_pixels(t, lanes):
             for ts in range(TUBE):
@@ -84,15 +88,15 @@ def tile_tubeletembedding_kernel(tc, video, W_words, W_scales, b, pos_embed, out
         w_codes = keep.tile([P, 4 * EMBED], U8, name="w_codes", align_bytes=64)
         load_pixels(0, 2)
         for quadrant in range(4):
-            nc.sync.dma_start(
-                out=w_scales[32 * quadrant : 32 * quadrant + 4, :].bitcast(I32),
-                in_=W_scales[0, 4 * quadrant : 4 * quadrant + 4, :].bitcast(I32),
+            nc.scalar.dma_start(
+                out=w_scales[32 * quadrant : 32 * quadrant + 4, :].bitcast(F32),
+                in_=W_scales[0, 4 * quadrant : 4 * quadrant + 4, :].bitcast(F32),
             )
-        nc.sync.dma_start(out=pos_bf[:, 0, :], in_=pos_bands[:, main_rows(0), :])
         nc.sync.dma_start(
             out=w_codes[:].bitcast(I32),
             in_=W_words[0].rearrange("p n t -> p (n t)").bitcast(I32),
         )
+        nc.sync.dma_start(out=pos_bf[:, 0, :], in_=pos_bands[:, main_rows(0), :])
         load_pixels(1, 1)
         nc.sync.dma_start(out=pos_bf[:, 1, :], in_=pos_bands[:, main_rows(1), :])
 
@@ -106,15 +110,17 @@ def tile_tubeletembedding_kernel(tc, video, W_words, W_scales, b, pos_embed, out
             )
             return acc
 
+        bias_all = keep.tile([P, EMBED], F32, name="bias_all")
         for h in range(2):
             nc.scalar.copy(out=addend[:, 0, half_cols(h)], in_=spread_rows(0, h)[:])
-        bias_all = [spread_rows(1, h) for h in range(2)]
+        for h in range(2):
+            nc.scalar.copy(out=bias_all[:, half_cols(h)], in_=spread_rows(1, h)[:])
 
         def make_addend(y):
             for h in range(2):
                 nc.vector.tensor_tensor(
-                    out=addend[:, 1 + y, half_cols(h)], in0=bias_all[h][:],
-                    in1=pos_bf[:, y, half_cols(h)], op=ADD,
+                    out=addend[:, 1 + y, half_cols(h)], in0=pos_bf[:, y, half_cols(h)],
+                    in1=bias_all[:, half_cols(h)], op=ADD,
                 )
 
         sorted_words = [
@@ -160,50 +166,65 @@ def tile_tubeletembedding_kernel(tc, video, W_words, W_scales, b, pos_embed, out
                 in_=flipped[:, :, :, il % 2 : P : 2].rearrange("p jj u q -> p q jj u"),
             )
 
-        def embed(tile_index, grouped, kind, rows):
+        token_tiles = [(grouped_pair[:].rearrange("p q v -> p (q v)"), 0, out_bands[:, 0:2, :])]
+        for y in range(2):
+            for batch in range(BATCH):
+                bands = slice(BATCH_BANDS * batch, BATCH_BANDS * (batch + 1))
+                token_tiles.append(
+                    (
+                        grouped_main[:, y, bands].rearrange("p q a v -> p (q a v)"),
+                        1 + y,
+                        out_bands[bands, main_rows(y), :],
+                    )
+                )
+
+        def start(tile_index):
             tokens = slice(P * tile_index, P * (tile_index + 1))
             nc.vector.quantize_mx(
-                out=x_codes[:, tokens].bitcast(FP8X4), scales=x_scales[:, tokens], in_=grouped
+                out=x_codes[:, tokens].bitcast(FP8X4),
+                scales=x_scales[:, tokens],
+                in_=token_tiles[tile_index][0],
             )
-            result = results.tile([P, EMBED], F32, name="result")
+            sums = []
             for h in range(2):
-                cols = half_cols(h)
                 acc = psum_acc.tile([P, N_HALF], F32, name="acc")
                 nc.tensor.matmul_mx(
                     out=acc[:],
                     lhsT=x_codes[:, tokens].bitcast(FP8X4),
                     lhsT_scale=x_scales[:, tokens],
                     rhs=w_codes[:, 4 * N_HALF * h : 4 * N_HALF * (h + 1)].bitcast(FP8X4),
-                    rhs_scale=w_scales[:, cols],
+                    rhs_scale=w_scales[:, half_cols(h)],
                     start=True,
                     stop=True,
                 )
+                sums.append(acc)
+            return sums
+
+        def finish(tile_index, sums):
+            kind = token_tiles[tile_index][1]
+            rows = token_tiles[tile_index][2]
+            result = results.tile([P, EMBED], F32, name="result")
+            for h in range(2):
+                cols = half_cols(h)
                 nc.vector.tensor_tensor(
-                    out=result[:, cols], in0=acc[:], in1=addend[:, kind, cols], op=ADD
+                    out=result[:, cols], in0=sums[h][:], in1=addend[:, kind, cols], op=ADD
                 )
                 nc.sync.dma_start(out=rows[:, :, cols], in_=result[:, cols])
-
-        def embed_main(y):
-            for batch in range(BATCH):
-                bands = slice(BATCH_BANDS * batch, BATCH_BANDS * (batch + 1))
-                embed(
-                    1 + BATCH * y + batch,
-                    grouped_main[:, y, bands].rearrange("p q a v -> p (q a v)"),
-                    1 + y,
-                    out_bands[bands, main_rows(y), :],
-                )
 
         sort_words(nc.vector.tensor_copy, 0)
         for jp in range(GRID // 2):
             flipped = flip(0, jp)
             for il in range(2):
                 gather_row_pair(il, jp, flipped)
-            if jp == 0:
-                embed(0, grouped_pair[:].rearrange("p q v -> p (q v)"), 0, out_bands[:, 0:2, :])
-                make_addend(0)
-        embed_main(0)
+        sums = start(0)
+        make_addend(0)
         sort_words(nc.scalar.copy, 1)
-        for jp in range(GRID // 2):
-            gather_row_pair(2, jp, flip(1, jp))
-        make_addend(1)
-        embed_main(1)
+        for tile_index in range(len(token_tiles)):
+            next_sums = start(tile_index + 1) if tile_index + 1 < len(token_tiles) else None
+            jp = tile_index - 1
+            if 0 <= jp < GRID // 2:
+                gather_row_pair(2, jp, flip(1, jp))
+            finish(tile_index, sums)
+            sums = next_sums
+            if tile_index == BATCH - 1:
+                make_addend(1)

@@ -69,13 +69,10 @@ def tile_tubeletembedding_kernel(tc, video, W_words, W_scales, b, pos_embed, out
         pixels = [keep.tile([P, TUBE, STRIP], BF16, name="pixels%d" % t) for t in range(2)]
         nc.vector.memset(pixels[1][:].bitcast(I32), 0)
 
-        nc.gpsimd.dma_start(
-            out=small_rows[BIAS_ROW : BIAS_ROW + 1, :].bitcast(F32),
-            in_=b.rearrange("(o n) -> o n", o=1).bitcast(F32),
+        nc.scalar.dma_start(
+            out=small_rows[BIAS_ROW : BIAS_ROW + 1, :], in_=b.rearrange("(o n) -> o n", o=1)
         )
-        nc.gpsimd.dma_start(
-            out=small_rows[0:32, :].bitcast(F32), in_=pos_bands[:, 0:2, :].bitcast(F32)
-        )
+        nc.scalar.dma_start(out=small_rows[0:32, :], in_=pos_bands[:, 0:2, :])
 
         def load_pixels(t, lanes):
             for ts in range(TUBE):
@@ -87,15 +84,15 @@ def tile_tubeletembedding_kernel(tc, video, W_words, W_scales, b, pos_embed, out
         pos_bf = keep.tile([P, 2, EMBED], BF16, name="pos_bf")
         w_codes = keep.tile([P, 4 * EMBED], U8, name="w_codes", align_bytes=64)
         load_pixels(0, 2)
+        nc.sync.dma_start(
+            out=w_codes[:].bitcast(I32),
+            in_=W_words[0].rearrange("p n t -> p (n t)").bitcast(I32),
+        )
         for quadrant in range(4):
             nc.scalar.dma_start(
                 out=w_scales[32 * quadrant : 32 * quadrant + 4, :].bitcast(F32),
                 in_=W_scales[0, 4 * quadrant : 4 * quadrant + 4, :].bitcast(F32),
             )
-        nc.sync.dma_start(
-            out=w_codes[:].bitcast(I32),
-            in_=W_words[0].rearrange("p n t -> p (n t)").bitcast(I32),
-        )
         nc.sync.dma_start(out=pos_bf[:, 0, :], in_=pos_bands[:, main_rows(0), :])
         load_pixels(1, 1)
         nc.sync.dma_start(out=pos_bf[:, 1, :], in_=pos_bands[:, main_rows(1), :])
@@ -116,9 +113,9 @@ def tile_tubeletembedding_kernel(tc, video, W_words, W_scales, b, pos_embed, out
         for h in range(2):
             nc.scalar.copy(out=bias_all[:, half_cols(h)], in_=spread_rows(1, h)[:])
 
-        def make_addend(y):
+        for y in range(2):
             for h in range(2):
-                nc.vector.tensor_tensor(
+                nc.gpsimd.tensor_tensor(
                     out=addend[:, 1 + y, half_cols(h)], in0=pos_bf[:, y, half_cols(h)],
                     in1=bias_all[:, half_cols(h)], op=ADD,
                 )
@@ -161,7 +158,8 @@ def tile_tubeletembedding_kernel(tc, video, W_words, W_scales, b, pos_embed, out
                 target = grouped_pair[:].bitcast(F32)
             else:
                 target = grouped_main[:].bitcast(F32)[:, (rp - 1) // 4, :, (rp - 1) % 4, :]
-            nc.scalar.copy(
+            copy = nc.vector.tensor_copy if rp in (1, 2) else nc.scalar.copy
+            copy(
                 out=target.rearrange("p q (jj u) -> p q jj u", u=2),
                 in_=flipped[:, :, :, il % 2 : P : 2].rearrange("p jj u q -> p q jj u"),
             )
@@ -212,12 +210,12 @@ def tile_tubeletembedding_kernel(tc, video, W_words, W_scales, b, pos_embed, out
                 nc.sync.dma_start(out=rows[:, :, cols], in_=result[:, cols])
 
         sort_words(nc.vector.tensor_copy, 0)
+        flipped = [flip(0, jp) for jp in range(GRID // 2)]
         for jp in range(GRID // 2):
-            flipped = flip(0, jp)
             for il in range(2):
-                gather_row_pair(il, jp, flipped)
-        sums = start(0)
-        make_addend(0)
+                gather_row_pair(il, jp, flipped[jp])
+            if jp == 0:
+                sums = start(0)
         sort_words(nc.scalar.copy, 1)
         for tile_index in range(len(token_tiles)):
             next_sums = start(tile_index + 1) if tile_index + 1 < len(token_tiles) else None
@@ -226,5 +224,3 @@ def tile_tubeletembedding_kernel(tc, video, W_words, W_scales, b, pos_embed, out
                 gather_row_pair(2, jp, flip(1, jp))
             finish(tile_index, sums)
             sums = next_sums
-            if tile_index == BATCH - 1:
-                make_addend(1)

@@ -204,9 +204,15 @@ def tile_tubeletembedding_kernel(tc, video, W_words, W_scales, b, pos_embed, out
             result = results.tile([P, EMBED], F32, name="result")
             for h in range(2):
                 cols = half_cols(h)
-                nc.vector.tensor_tensor(
-                    out=result[:, cols], in0=sums[h][:], in1=addend[:, kind, cols], op=ADD
-                )
+                if h == 1 and tile_index % 2 == 0 and 0 < tile_index < len(token_tiles) - 1:
+                    nc.scalar.copy(out=result[:, cols], in_=sums[h][:])
+                    nc.gpsimd.tensor_tensor(
+                        out=result[:, cols], in0=result[:, cols], in1=addend[:, kind, cols], op=ADD
+                    )
+                else:
+                    nc.vector.tensor_tensor(
+                        out=result[:, cols], in0=sums[h][:], in1=addend[:, kind, cols], op=ADD
+                    )
                 nc.sync.dma_start(out=rows[:, :, cols], in_=result[:, cols])
 
         sort_words(nc.vector.tensor_copy, 0)
@@ -219,8 +225,8 @@ def tile_tubeletembedding_kernel(tc, video, W_words, W_scales, b, pos_embed, out
         sort_words(nc.scalar.copy, 1)
         for tile_index in range(len(token_tiles)):
             next_sums = start(tile_index + 1) if tile_index + 1 < len(token_tiles) else None
+            finish(tile_index, sums)
+            sums = next_sums
             jp = tile_index - 1
             if 0 <= jp < GRID // 2:
                 gather_row_pair(2, jp, flip(1, jp))
-            finish(tile_index, sums)
-            sums = next_sums

@@ -54,7 +54,7 @@ def tile_tubeletembedding_kernel(tc, video, W_words, W_scales, b, pos_embed, out
             return slice(N_HALF * h, N_HALF * (h + 1))
 
         small_rows = keep.tile([P, EMBED], BF16, name="small_rows")
-        nc.vector.memset(small_rows[:], 0.0)
+        nc.vector.memset(small_rows[:].bitcast(I32), 0)
         w_scales = keep.tile([P, EMBED], U8, name="w_scales", align_bytes=64)
         nc.vector.memset(w_scales[:].bitcast(I32), 0)
         identity = keep.tile([P, P], F32, name="identity")
@@ -69,10 +69,10 @@ def tile_tubeletembedding_kernel(tc, video, W_words, W_scales, b, pos_embed, out
         pixels = [keep.tile([P, TUBE, STRIP], BF16, name="pixels%d" % t) for t in range(2)]
         nc.vector.memset(pixels[1][:].bitcast(I32), 0)
 
-        nc.scalar.dma_start(
+        nc.sync.dma_start(
             out=small_rows[BIAS_ROW : BIAS_ROW + 1, :], in_=b.rearrange("(o n) -> o n", o=1)
         )
-        nc.scalar.dma_start(out=small_rows[0:32, :], in_=pos_bands[:, 0:2, :])
+        nc.sync.dma_start(out=small_rows[0:32, :], in_=pos_bands[:, 0:2, :])
 
         def load_pixels(t, lanes):
             for ts in range(TUBE):
@@ -84,16 +84,16 @@ def tile_tubeletembedding_kernel(tc, video, W_words, W_scales, b, pos_embed, out
         pos_bf = keep.tile([P, 2, EMBED], BF16, name="pos_bf")
         w_codes = keep.tile([P, 4 * EMBED], U8, name="w_codes", align_bytes=64)
         load_pixels(0, 2)
+        nc.sync.dma_start(out=pos_bf[:, 0, :], in_=pos_bands[:, main_rows(0), :])
         nc.sync.dma_start(
             out=w_codes[:].bitcast(I32),
             in_=W_words[0].rearrange("p n t -> p (n t)").bitcast(I32),
         )
         for quadrant in range(4):
-            nc.scalar.dma_start(
-                out=w_scales[32 * quadrant : 32 * quadrant + 4, :].bitcast(F32),
-                in_=W_scales[0, 4 * quadrant : 4 * quadrant + 4, :].bitcast(F32),
+            nc.sync.dma_start(
+                out=w_scales[32 * quadrant : 32 * quadrant + 4, :].bitcast(I32),
+                in_=W_scales[0, 4 * quadrant : 4 * quadrant + 4, :].bitcast(I32),
             )
-        nc.sync.dma_start(out=pos_bf[:, 0, :], in_=pos_bands[:, main_rows(0), :])
         load_pixels(1, 1)
         nc.sync.dma_start(out=pos_bf[:, 1, :], in_=pos_bands[:, main_rows(1), :])
 
@@ -109,16 +109,18 @@ def tile_tubeletembedding_kernel(tc, video, W_words, W_scales, b, pos_embed, out
 
         bias_all = keep.tile([P, EMBED], F32, name="bias_all")
         for h in range(2):
-            nc.scalar.copy(out=addend[:, 0, half_cols(h)], in_=spread_rows(0, h)[:])
-        for h in range(2):
             nc.scalar.copy(out=bias_all[:, half_cols(h)], in_=spread_rows(1, h)[:])
+        for h in range(2):
+            nc.scalar.copy(out=addend[:, 0, half_cols(h)], in_=spread_rows(0, h)[:])
 
-        for y in range(2):
+        def make_addend(engine, y):
             for h in range(2):
-                nc.gpsimd.tensor_tensor(
+                engine.tensor_tensor(
                     out=addend[:, 1 + y, half_cols(h)], in0=pos_bf[:, y, half_cols(h)],
                     in1=bias_all[:, half_cols(h)], op=ADD,
                 )
+
+        make_addend(nc.gpsimd, 1)
 
         sorted_words = [
             keep.tile([P, GRID, 2, P], F32, name="sorted_words%d" % t) for t in range(2)
@@ -164,25 +166,20 @@ def tile_tubeletembedding_kernel(tc, video, W_words, W_scales, b, pos_embed, out
                 in_=flipped[:, :, :, il % 2 : P : 2].rearrange("p jj u q -> p q jj u"),
             )
 
-        token_tiles = [(grouped_pair[:].rearrange("p q v -> p (q v)"), 0, out_bands[:, 0:2, :])]
+        token_tiles = [(0, out_bands[:, 0:2, :])]
         for y in range(2):
             for batch in range(BATCH):
                 bands = slice(BATCH_BANDS * batch, BATCH_BANDS * (batch + 1))
-                token_tiles.append(
-                    (
-                        grouped_main[:, y, bands].rearrange("p q a v -> p (q a v)"),
-                        1 + y,
-                        out_bands[bands, main_rows(y), :],
-                    )
-                )
+                token_tiles.append((1 + y, out_bands[bands, main_rows(y), :]))
+
+        def quantise(first_tile, grouped):
+            tokens = slice(P * first_tile, P * first_tile + grouped.shape[1] // 4)
+            nc.vector.quantize_mx(
+                out=x_codes[:, tokens].bitcast(FP8X4), scales=x_scales[:, tokens], in_=grouped
+            )
 
         def start(tile_index):
             tokens = slice(P * tile_index, P * (tile_index + 1))
-            nc.vector.quantize_mx(
-                out=x_codes[:, tokens].bitcast(FP8X4),
-                scales=x_scales[:, tokens],
-                in_=token_tiles[tile_index][0],
-            )
             sums = []
             for h in range(2):
                 acc = psum_acc.tile([P, N_HALF], F32, name="acc")
@@ -199,34 +196,35 @@ def tile_tubeletembedding_kernel(tc, video, W_words, W_scales, b, pos_embed, out
             return sums
 
         def finish(tile_index, sums):
-            kind = token_tiles[tile_index][1]
-            rows = token_tiles[tile_index][2]
+            kind = token_tiles[tile_index][0]
+            rows = token_tiles[tile_index][1]
             result = results.tile([P, EMBED], F32, name="result")
             for h in range(2):
                 cols = half_cols(h)
-                if h == 1 and tile_index % 2 == 0 and 0 < tile_index < len(token_tiles) - 1:
-                    nc.scalar.copy(out=result[:, cols], in_=sums[h][:])
-                    nc.gpsimd.tensor_tensor(
-                        out=result[:, cols], in0=result[:, cols], in1=addend[:, kind, cols], op=ADD
-                    )
-                else:
-                    nc.vector.tensor_tensor(
-                        out=result[:, cols], in0=sums[h][:], in1=addend[:, kind, cols], op=ADD
-                    )
+                nc.vector.tensor_tensor(
+                    out=result[:, cols], in0=sums[h][:], in1=addend[:, kind, cols], op=ADD
+                )
                 nc.sync.dma_start(out=rows[:, :, cols], in_=result[:, cols])
 
         sort_words(nc.vector.tensor_copy, 0)
+        make_addend(nc.vector, 0)
         flipped = [flip(0, jp) for jp in range(GRID // 2)]
         for jp in range(GRID // 2):
             for il in range(2):
                 gather_row_pair(il, jp, flipped[jp])
             if jp == 0:
+                quantise(0, grouped_pair[:].rearrange("p q v -> p (q v)"))
                 sums = start(0)
         sort_words(nc.scalar.copy, 1)
         for tile_index in range(len(token_tiles)):
-            next_sums = start(tile_index + 1) if tile_index + 1 < len(token_tiles) else None
-            finish(tile_index, sums)
-            sums = next_sums
+            next_sums = None
+            if tile_index + 1 < len(token_tiles):
+                if tile_index % BATCH == 0:
+                    y = tile_index // BATCH
+                    quantise(tile_index + 1, grouped_main[:, y].rearrange("p q a v -> p (q a v)"))
+                next_sums = start(tile_index + 1)
             jp = tile_index - 1
             if 0 <= jp < GRID // 2:
                 gather_row_pair(2, jp, flip(1, jp))
+            finish(tile_index, sums)
+            sums = next_sums

@@ -69,21 +69,20 @@ def tile_tubeletembedding_kernel(tc, video, W_words, W_scales, b, pos_embed, out
         pixels = [keep.tile([P, TUBE, STRIP], BF16, name="pixels%d" % t) for t in range(2)]
         nc.vector.memset(pixels[1][:].bitcast(I32), 0)
 
+        def load_pixels(t, lanes, ts):
+            for lane in range(lanes):
+                nc.sync.dma_start(
+                    out=pixels[t][lane:P:2, ts, :], in_=strips[:, ts, :, 2 * t + lane, :]
+                )
+
+        pos_bf = keep.tile([P, 2, EMBED], BF16, name="pos_bf")
+        w_codes = keep.tile([P, 4 * EMBED], U8, name="w_codes", align_bytes=64)
+        load_pixels(0, 2, 0)
         nc.sync.dma_start(
             out=small_rows[BIAS_ROW : BIAS_ROW + 1, :], in_=b.rearrange("(o n) -> o n", o=1)
         )
         nc.sync.dma_start(out=small_rows[0:32, :], in_=pos_bands[:, 0:2, :])
-
-        def load_pixels(t, lanes):
-            for ts in range(TUBE):
-                for lane in range(lanes):
-                    nc.sync.dma_start(
-                        out=pixels[t][lane:P:2, ts, :], in_=strips[:, ts, :, 2 * t + lane, :]
-                    )
-
-        pos_bf = keep.tile([P, 2, EMBED], BF16, name="pos_bf")
-        w_codes = keep.tile([P, 4 * EMBED], U8, name="w_codes", align_bytes=64)
-        load_pixels(0, 2)
+        load_pixels(0, 2, 1)
         nc.sync.dma_start(out=pos_bf[:, 0, :], in_=pos_bands[:, main_rows(0), :])
         nc.sync.dma_start(
             out=w_codes[:].bitcast(I32),
@@ -94,7 +93,8 @@ def tile_tubeletembedding_kernel(tc, video, W_words, W_scales, b, pos_embed, out
                 out=w_scales[32 * quadrant : 32 * quadrant + 4, :].bitcast(I32),
                 in_=W_scales[0, 4 * quadrant : 4 * quadrant + 4, :].bitcast(I32),
             )
-        load_pixels(1, 1)
+        for ts in range(TUBE):
+            load_pixels(1, 1, ts)
         nc.sync.dma_start(out=pos_bf[:, 1, :], in_=pos_bands[:, main_rows(1), :])
 
         addend = keep.tile([P, 3, EMBED], F32, name="addend")
@@ -130,20 +130,16 @@ def tile_tubeletembedding_kernel(tc, video, W_words, W_scales, b, pos_embed, out
         x_codes = keep.tile([P, TOKENS], U32, name="x_codes", align_bytes=64)
         x_scales = keep.tile([P, TOKENS], U8, name="x_scales", align_bytes=64)
 
-        def sort_words(copy, t):
-            for ts in range(TUBE):
-                half = slice(ts * (P // 2), (ts + 1) * (P // 2))
-                by_column = pixels[t][:, ts, :].bitcast(F32).rearrange(
-                    "p (py j q u) -> p j u py q", py=PATCH, j=GRID, q=4, u=2
-                )
-                for jp in range(GRID // 2):
-                    pair = slice(2 * jp, 2 * jp + 2)
-                    copy(
-                        out=sorted_words[t][:, pair, :, half].rearrange(
-                            "p j u (py q) -> p j u py q", q=4
-                        ),
-                        in_=by_column[:, pair],
-                    )
+        def sort_words(copy, t, ts, jp):
+            half = slice(ts * (P // 2), (ts + 1) * (P // 2))
+            by_column = pixels[t][:, ts, :].bitcast(F32).rearrange(
+                "p (py j q u) -> p j u py q", py=PATCH, j=GRID, q=4, u=2
+            )
+            pair = slice(2 * jp, 2 * jp + 2)
+            copy(
+                out=sorted_words[t][:, pair, :, half].rearrange("p j u (py q) -> p j u py q", q=4),
+                in_=by_column[:, pair],
+            )
 
         def flip(t, jp):
             flipped = psum_flip.tile([P, 2, 2, P], F32, name="flipped")
@@ -195,18 +191,36 @@ def tile_tubeletembedding_kernel(tc, video, W_words, W_scales, b, pos_embed, out
                 sums.append(acc)
             return sums
 
-        def finish(tile_index, sums):
+        side_tiles = (1, 3, 5, 6)
+        late_stores = []
+
+        def side_half(tile_index, sums, result):
+            cols = half_cols(1)
+            kind = token_tiles[tile_index][0]
+            nc.scalar.copy(out=result[:, cols], in_=sums[1][:])
+            nc.gpsimd.tensor_tensor(
+                out=result[:, cols], in0=result[:, cols], in1=addend[:, kind, cols], op=ADD
+            )
+            late_stores.append((tile_index, token_tiles[tile_index][1][:, :, cols], result[:, cols]))
+
+        def finish(tile_index, sums, result):
             kind = token_tiles[tile_index][0]
             rows = token_tiles[tile_index][1]
-            result = results.tile([P, EMBED], F32, name="result")
-            for h in range(2):
+            for h in range(1 if tile_index in side_tiles else 2):
                 cols = half_cols(h)
                 nc.vector.tensor_tensor(
                     out=result[:, cols], in0=sums[h][:], in1=addend[:, kind, cols], op=ADD
                 )
                 nc.sync.dma_start(out=rows[:, :, cols], in_=result[:, cols])
+            last = tile_index == len(token_tiles) - 1
+            for entry in list(late_stores):
+                if last or entry[0] + 2 <= tile_index:
+                    nc.sync.dma_start(out=entry[1], in_=entry[2])
+                    late_stores.remove(entry)
 
-        sort_words(nc.vector.tensor_copy, 0)
+        for ts in range(TUBE):
+            for jp in range(GRID // 2):
+                sort_words(nc.vector.tensor_copy, 0, ts, jp)
         make_addend(nc.vector, 0)
         flipped = [flip(0, jp) for jp in range(GRID // 2)]
         for jp in range(GRID // 2):
@@ -215,7 +229,9 @@ def tile_tubeletembedding_kernel(tc, video, W_words, W_scales, b, pos_embed, out
             if jp == 0:
                 quantise(0, grouped_pair[:].rearrange("p q v -> p (q v)"))
                 sums = start(0)
-        sort_words(nc.scalar.copy, 1)
+        for jp in range(GRID // 2):
+            for ts in range(TUBE):
+                sort_words(nc.scalar.copy, 1, ts, jp)
         for tile_index in range(len(token_tiles)):
             next_sums = None
             if tile_index + 1 < len(token_tiles):
@@ -223,8 +239,11 @@ def tile_tubeletembedding_kernel(tc, video, W_words, W_scales, b, pos_embed, out
                     y = tile_index // BATCH
                     quantise(tile_index + 1, grouped_main[:, y].rearrange("p q a v -> p (q a v)"))
                 next_sums = start(tile_index + 1)
-            jp = tile_index - 1
-            if 0 <= jp < GRID // 2:
-                gather_row_pair(2, jp, flip(1, jp))
-            finish(tile_index, sums)
+            result = results.tile([P, EMBED], F32, name="result")
+            if tile_index in side_tiles:
+                side_half(tile_index, sums, result)
+            if tile_index == 1:
+                for jp in range(GRID // 2):
+                    gather_row_pair(2, jp, flip(1, jp))
+            finish(tile_index, sums, result)
             sums = next_sums

@@ -55,6 +55,13 @@ def tile_tubeletembedding_kernel(tc, video, W_words, W_scales, b, pos_embed, out
 
         small_rows = keep.tile([P, EMBED], BF16, name="small_rows")
         nc.vector.memset(small_rows[:].bitcast(I32), 0)
+        zeros = keep.tile([P, N_HALF], BF16, name="zeros")
+        nc.vector.memset(zeros[:], 0.0)
+        warm_up = psum_acc.tile([P, N_HALF], F32, name="acc")
+        for repeat in range(3):
+            nc.tensor.matmul(
+                out=warm_up[:], lhsT=zeros[:, 0:P], rhs=zeros[:], start=True, stop=True
+            )
         w_scales = keep.tile([P, EMBED], U8, name="w_scales", align_bytes=64)
         nc.vector.memset(w_scales[:].bitcast(I32), 0)
         identity = keep.tile([P, P], F32, name="identity")
@@ -107,20 +114,11 @@ def tile_tubeletembedding_kernel(tc, video, W_words, W_scales, b, pos_embed, out
             )
             return acc
 
-        bias_all = keep.tile([P, EMBED], F32, name="bias_all")
-        for h in range(2):
-            nc.scalar.copy(out=bias_all[:, half_cols(h)], in_=spread_rows(1, h)[:])
         for h in range(2):
             nc.scalar.copy(out=addend[:, 0, half_cols(h)], in_=spread_rows(0, h)[:])
-
-        def make_addend(engine, y):
-            for h in range(2):
-                engine.tensor_tensor(
-                    out=addend[:, 1 + y, half_cols(h)], in0=pos_bf[:, y, half_cols(h)],
-                    in1=bias_all[:, half_cols(h)], op=ADD,
-                )
-
-        make_addend(nc.gpsimd, 1)
+        bias_banks = [spread_rows(1, h) for h in range(2)]
+        bias_all = keep.tile([P, EMBED], F32, name="bias_all")
+        nc.scalar.copy(out=bias_all[:, half_cols(0)], in_=bias_banks[0][:])
 
         sorted_words = [
             keep.tile([P, GRID, 2, P], F32, name="sorted_words%d" % t) for t in range(2)
@@ -156,8 +154,7 @@ def tile_tubeletembedding_kernel(tc, video, W_words, W_scales, b, pos_embed, out
                 target = grouped_pair[:].bitcast(F32)
             else:
                 target = grouped_main[:].bitcast(F32)[:, (rp - 1) // 4, :, (rp - 1) % 4, :]
-            copy = nc.vector.tensor_copy if rp in (1, 2) else nc.scalar.copy
-            copy(
+            nc.scalar.copy(
                 out=target.rearrange("p q (jj u) -> p q jj u", u=2),
                 in_=flipped[:, :, :, il % 2 : P : 2].rearrange("p jj u q -> p q jj u"),
             )
@@ -191,7 +188,7 @@ def tile_tubeletembedding_kernel(tc, video, W_words, W_scales, b, pos_embed, out
                 sums.append(acc)
             return sums
 
-        side_tiles = (1, 3, 5, 6)
+        side_tiles = ()
         late_stores = []
 
         def side_half(tile_index, sums, result):
@@ -203,47 +200,67 @@ def tile_tubeletembedding_kernel(tc, video, W_words, W_scales, b, pos_embed, out
             )
             late_stores.append((tile_index, token_tiles[tile_index][1][:, :, cols], result[:, cols]))
 
-        def finish(tile_index, sums, result):
+        def finish(tile_index, h, sums, result):
             kind = token_tiles[tile_index][0]
             rows = token_tiles[tile_index][1]
-            for h in range(1 if tile_index in side_tiles else 2):
-                cols = half_cols(h)
-                nc.vector.tensor_tensor(
-                    out=result[:, cols], in0=sums[h][:], in1=addend[:, kind, cols], op=ADD
-                )
-                nc.sync.dma_start(out=rows[:, :, cols], in_=result[:, cols])
+            cols = half_cols(h)
+            nc.vector.tensor_tensor(
+                out=result[:, cols], in0=sums[h][:], in1=addend[:, kind, cols], op=ADD
+            )
+            nc.sync.dma_start(out=rows[:, :, cols], in_=result[:, cols])
+
+        def first_addend(h):
+            cols = half_cols(h)
+            nc.vector.tensor_tensor(
+                out=addend[:, 1, cols], in0=bias_banks[h][:], in1=pos_bf[:, 0, cols], op=ADD
+            )
+
+        for ts in range(TUBE):
+            for jp in range(GRID // 2):
+                sort_words(nc.vector.tensor_copy, 0, ts, jp)
+        flipped = [flip(0, jp) for jp in range(GRID // 2)]
+        first_addend(0)
+        gather_row_pair(0, 0, flipped[0])
+        quantise(0, grouped_pair[:].rearrange("p q v -> p (q v)"))
+        first_addend(1)
+        sums = start(0)
+        for il, jp in ((1, 0), (0, 1), (1, 1), (0, 2)):
+            gather_row_pair(il, jp, flipped[jp])
+        result = results.tile([P, EMBED], F32, name="result")
+        finish(0, 0, sums, result)
+        quantise(1, grouped_main[:, 0].rearrange("p q a v -> p (q a v)"))
+        nc.scalar.copy(out=bias_all[:, half_cols(1)], in_=bias_banks[1][:])
+        gather_row_pair(1, 2, flipped[2])
+        for h in range(2):
+            nc.gpsimd.tensor_tensor(
+                out=addend[:, 2, half_cols(h)], in0=pos_bf[:, 1, half_cols(h)],
+                in1=bias_all[:, half_cols(h)], op=ADD,
+            )
+        for jp in range(GRID // 2):
+            for ts in range(TUBE):
+                sort_words(nc.scalar.copy, 1, ts, jp)
+        next_sums = start(1)
+        finish(0, 1, sums, result)
+        sums = next_sums
+        late_flips = {1: (0,), 2: (1, 2)}
+        for tile_index in range(1, len(token_tiles)):
+            next_sums = None
+            result = results.tile([P, EMBED], F32, name="result")
+            if tile_index == BATCH:
+                finish(tile_index, 0, sums, result)
+                quantise(BATCH + 1, grouped_main[:, 1].rearrange("p q a v -> p (q a v)"))
+            if tile_index + 1 < len(token_tiles):
+                next_sums = start(tile_index + 1)
+            if tile_index in side_tiles:
+                side_half(tile_index, sums, result)
+            for jp in late_flips.get(tile_index, ()):
+                gather_row_pair(2, jp, flip(1, jp))
+            for h in range(2):
+                if (tile_index, h) != (BATCH, 0) and not (h == 1 and tile_index in side_tiles):
+                    finish(tile_index, h, sums, result)
             last = tile_index == len(token_tiles) - 1
             for entry in list(late_stores):
                 if last or entry[0] + 2 <= tile_index:
                     nc.sync.dma_start(out=entry[1], in_=entry[2])
                     late_stores.remove(entry)
-
-        for ts in range(TUBE):
-            for jp in range(GRID // 2):
-                sort_words(nc.vector.tensor_copy, 0, ts, jp)
-        make_addend(nc.vector, 0)
-        flipped = [flip(0, jp) for jp in range(GRID // 2)]
-        for jp in range(GRID // 2):
-            for il in range(2):
-                gather_row_pair(il, jp, flipped[jp])
-            if jp == 0:
-                quantise(0, grouped_pair[:].rearrange("p q v -> p (q v)"))
-                sums = start(0)
-        for jp in range(GRID // 2):
-            for ts in range(TUBE):
-                sort_words(nc.scalar.copy, 1, ts, jp)
-        for tile_index in range(len(token_tiles)):
-            next_sums = None
-            if tile_index + 1 < len(token_tiles):
-                if tile_index % BATCH == 0:
-                    y = tile_index // BATCH
-                    quantise(tile_index + 1, grouped_main[:, y].rearrange("p q a v -> p (q a v)"))
-                next_sums = start(tile_index + 1)
-            result = results.tile([P, EMBED], F32, name="result")
-            if tile_index in side_tiles:
-                side_half(tile_index, sums, result)
-            if tile_index == 1:
-                for jp in range(GRID // 2):
-                    gather_row_pair(2, jp, flip(1, jp))
-            finish(tile_index, sums, result)
             sums = next_sums

@@ -188,7 +188,7 @@ def tile_tubeletembedding_kernel(tc, video, W_words, W_scales, b, pos_embed, out
                 sums.append(acc)
             return sums
 
-        side_tiles = ()
+        side_tiles = (3, 4, 5, 6)
         late_stores = []
 
         def side_half(tile_index, sums, result):

@@ -55,13 +55,6 @@ def tile_tubeletembedding_kernel(tc, video, W_words, W_scales, b, pos_embed, out
 
         small_rows = keep.tile([P, EMBED], BF16, name="small_rows")
         nc.vector.memset(small_rows[:].bitcast(I32), 0)
-        zeros = keep.tile([P, N_HALF], BF16, name="zeros")
-        nc.vector.memset(zeros[:], 0.0)
-        warm_up = psum_acc.tile([P, N_HALF], F32, name="acc")
-        for repeat in range(3):
-            nc.tensor.matmul(
-                out=warm_up[:], lhsT=zeros[:, 0:P], rhs=zeros[:], start=True, stop=True
-            )
         w_scales = keep.tile([P, EMBED], U8, name="w_scales", align_bytes=64)
         nc.vector.memset(w_scales[:].bitcast(I32), 0)
         identity = keep.tile([P, P], F32, name="identity")
@@ -198,7 +191,11 @@ def tile_tubeletembedding_kernel(tc, video, W_words, W_scales, b, pos_embed, out
             nc.gpsimd.tensor_tensor(
                 out=result[:, cols], in0=result[:, cols], in1=addend[:, kind, cols], op=ADD
             )
-            late_stores.append((tile_index, token_tiles[tile_index][1][:, :, cols], result[:, cols]))
+            late_stores.append((token_tiles[tile_index][1][:, :, cols], result[:, cols]))
+            if len(late_stores) > 1:
+                entry = late_stores[0]
+                late_stores.remove(entry)
+                nc.scalar.dma_start(out=entry[0], in_=entry[1])
 
         def finish(tile_index, h, sums, result):
             kind = token_tiles[tile_index][0]
@@ -258,9 +255,6 @@ def tile_tubeletembedding_kernel(tc, video, W_words, W_scales, b, pos_embed, out
             for h in range(2):
                 if (tile_index, h) != (BATCH, 0) and not (h == 1 and tile_index in side_tiles):
                     finish(tile_index, h, sums, result)
-            last = tile_index == len(token_tiles) - 1
-            for entry in list(late_stores):
-                if last or entry[0] + 2 <= tile_index:
-                    nc.sync.dma_start(out=entry[1], in_=entry[2])
-                    late_stores.remove(entry)
             sums = next_sums
+        for target, source in late_stores:
+            nc.scalar.dma_start(out=target, in_=source)

@@ -111,7 +111,6 @@ def tile_tubeletembedding_kernel(tc, video, W_words, W_scales, b, pos_embed, out
             nc.scalar.copy(out=addend[:, 0, half_cols(h)], in_=spread_rows(0, h)[:])
         bias_banks = [spread_rows(1, h) for h in range(2)]
         bias_all = keep.tile([P, EMBED], F32, name="bias_all")
-        nc.scalar.copy(out=bias_all[:, half_cols(0)], in_=bias_banks[0][:])
 
         sorted_words = [
             keep.tile([P, GRID, 2, P], F32, name="sorted_words%d" % t) for t in range(2)
@@ -226,7 +225,8 @@ def tile_tubeletembedding_kernel(tc, video, W_words, W_scales, b, pos_embed, out
         result = results.tile([P, EMBED], F32, name="result")
         finish(0, 0, sums, result)
         quantise(1, grouped_main[:, 0].rearrange("p q a v -> p (q a v)"))
-        nc.scalar.copy(out=bias_all[:, half_cols(1)], in_=bias_banks[1][:])
+        for h in range(2):
+            nc.scalar.copy(out=bias_all[:, half_cols(h)], in_=bias_banks[h][:])
         gather_row_pair(1, 2, flipped[2])
         for h in range(2):
             nc.gpsimd.tensor_tensor(

@@ -109,8 +109,13 @@ def tile_tubeletembedding_kernel(tc, video, W_words, W_scales, b, pos_embed, out
 
         for h in range(2):
             nc.scalar.copy(out=addend[:, 0, half_cols(h)], in_=spread_rows(0, h)[:])
-        bias_banks = [spread_rows(1, h) for h in range(2)]
-        bias_all = keep.tile([P, EMBED], F32, name="bias_all")
+        bias_bank = psum_acc.tile([P, EMBED], BF16, name="acc")
+        for h in range(2):
+            nc.tensor.matmul(
+                out=bias_bank[:, half_cols(h)], lhsT=pickers[:, 1, :],
+                rhs=small_rows[:, half_cols(h)], start=True, stop=True,
+            )
+        bias_all = keep.tile([P, EMBED], BF16, name="bias_all")
 
         sorted_words = [
             keep.tile([P, GRID, 2, P], F32, name="sorted_words%d" % t) for t in range(2)
@@ -208,7 +213,7 @@ def tile_tubeletembedding_kernel(tc, video, W_words, W_scales, b, pos_embed, out
         def first_addend(h):
             cols = half_cols(h)
             nc.vector.tensor_tensor(
-                out=addend[:, 1, cols], in0=bias_banks[h][:], in1=pos_bf[:, 0, cols], op=ADD
+                out=addend[:, 1, cols], in0=bias_bank[:, cols], in1=pos_bf[:, 0, cols], op=ADD
             )
 
         for ts in range(TUBE):
@@ -225,8 +230,7 @@ def tile_tubeletembedding_kernel(tc, video, W_words, W_scales, b, pos_embed, out
         result = results.tile([P, EMBED], F32, name="result")
         finish(0, 0, sums, result)
         quantise(1, grouped_main[:, 0].rearrange("p q a v -> p (q a v)"))
-        for h in range(2):
-            nc.scalar.copy(out=bias_all[:, half_cols(h)], in_=bias_banks[h][:])
+        nc.scalar.copy(out=bias_all[:], in_=bias_bank[:])
         gather_row_pair(1, 2, flipped[2])
         for h in range(2):
             nc.gpsimd.tensor_tensor(

from contextlib import ExitStack

import concourse.mybir as mybir
from concourse.masks import make_identity

F32 = mybir.dt.float32
BF16 = mybir.dt.bfloat16
I32 = mybir.dt.int32
U32 = mybir.dt.uint32
U8 = mybir.dt.uint8
FP8X4 = mybir.dt.float8_e4m3fn_x4
ADD = mybir.AluOpType.add

P = 128
BATCH = 4
TUBES = 8
TUBE = 2
GRID = 6
PATCH = 16
EMBED = 1024
K = TUBE * PATCH * PATCH
BANDS = BATCH * TUBES * 2
BATCH_BANDS = BANDS // BATCH
BAND_GRID_ROWS = GRID // 2
BAND_ROWS = BAND_GRID_ROWS * GRID
STRIP = PATCH * GRID * PATCH
N_HALF = 512
MAIN_ROWS = 8
TOKENS = BATCH * TUBES * GRID * GRID
BIAS_ROW = 32
FLOPS = 2 * TOKENS * K * EMBED


def tile_tubeletembedding_kernel(tc, video, W_words, W_scales, b, pos_embed, out):
    nc = tc.nc
    with ExitStack() as ctx:
        keep = ctx.enter_context(tc.tile_pool(name="keep", bufs=1))
        results = ctx.enter_context(tc.tile_pool(name="results", bufs=TOKENS // P))
        psum_flip = ctx.enter_context(tc.psum_pool(name="psum_flip", bufs=3))
        psum_acc = ctx.enter_context(tc.psum_pool(name="psum_acc", bufs=5))
        ctx.enter_context(tc.manual_schedule())

        strips = video[:, :, 0, :, :].rearrange(
            "b (d ts) (half il py) w -> (b d) ts half il (py w)",
            ts=TUBE, half=2, il=BAND_GRID_ROWS, py=PATCH,
        )
        pos_bands = pos_embed[0].rearrange("(q r) n -> q r n", r=BAND_ROWS)
        out_bands = out.rearrange("b (q r) n -> (b q) r n", r=BAND_ROWS)

        def main_rows(y):
            return slice(2 + MAIN_ROWS * y, 2 + MAIN_ROWS * (y + 1))

        def half_cols(h):
            return slice(N_HALF * h, N_HALF * (h + 1))

        small_rows = keep.tile([P, EMBED], BF16, name="small_rows")
        nc.vector.memset(small_rows[:].bitcast(I32), 0)
        w_scales = keep.tile([P, EMBED], U8, name="w_scales", align_bytes=64)
        nc.vector.memset(w_scales[:].bitcast(I32), 0)
        identity = keep.tile([P, P], F32, name="identity")
        make_identity(nc, identity[:])
        pickers = keep.tile([P, 2, P], BF16, name="pickers")
        nc.vector.memset(pickers[:], 0.0)
        nc.vector.memset(pickers[BIAS_ROW : BIAS_ROW + 1, :, :], 1.0)
        nc.vector.tensor_copy(
            out=pickers[0:32, 0, :].rearrange("k (c m) -> k c m", m=32),
            in_=identity[0:32, 0:32].unsqueeze(1).to_broadcast([32, BATCH, 32]),
        )
        pixels = [keep.tile([P, TUBE, STRIP], BF16, name="pixels%d" % t) for t in range(2)]
        nc.vector.memset(pixels[1][:].bitcast(I32), 0)

        def load_pixels(t, lanes, ts):
            for lane in range(lanes):
                nc.sync.dma_start(
                    out=pixels[t][lane:P:2, ts, :], in_=strips[:, ts, :, 2 * t + lane, :]
                )

        pos_bf = keep.tile([P, 2, EMBED], BF16, name="pos_bf")
        w_codes = keep.tile([P, 4 * EMBED], U8, name="w_codes", align_bytes=64)
        load_pixels(0, 2, 0)
        nc.sync.dma_start(
            out=small_rows[BIAS_ROW : BIAS_ROW + 1, :], in_=b.rearrange("(o n) -> o n", o=1)
        )
        nc.sync.dma_start(out=small_rows[0:32, :], in_=pos_bands[:, 0:2, :])
        load_pixels(0, 2, 1)
        nc.sync.dma_start(out=pos_bf[:, 0, :], in_=pos_bands[:, main_rows(0), :])
        nc.sync.dma_start(
            out=w_codes[:].bitcast(I32),
            in_=W_words[0].rearrange("p n t -> p (n t)").bitcast(I32),
        )
        for quadrant in range(4):
            nc.sync.dma_start(
                out=w_scales[32 * quadrant : 32 * quadrant + 4, :].bitcast(I32),
                in_=W_scales[0, 4 * quadrant : 4 * quadrant + 4, :].bitcast(I32),
            )
        for ts in range(TUBE):
            load_pixels(1, 1, ts)
        nc.sync.dma_start(out=pos_bf[:, 1, :], in_=pos_bands[:, main_rows(1), :])

        addend = keep.tile([P, 3, EMBED], F32, name="addend")

        def spread_rows(picker, h):
            acc = psum_acc.tile([P, N_HALF], F32, name="acc")
            nc.tensor.matmul(
                out=acc[:], lhsT=pickers[:, picker, :], rhs=small_rows[:, half_cols(h)],
                start=True, stop=True,
            )
            return acc

        for h in range(2):
            nc.scalar.copy(out=addend[:, 0, half_cols(h)], in_=spread_rows(0, h)[:])
        bias_bank = psum_acc.tile([P, EMBED], BF16, name="acc")
        for h in range(2):
            nc.tensor.matmul(
                out=bias_bank[:, half_cols(h)], lhsT=pickers[:, 1, :],
                rhs=small_rows[:, half_cols(h)], start=True, stop=True,
            )
        bias_all = keep.tile([P, EMBED], BF16, name="bias_all")

        sorted_words = [
            keep.tile([P, GRID, 2, P], F32, name="sorted_words%d" % t) for t in range(2)
        ]
        grouped_pair = keep.tile([P, BANDS, 8], BF16, name="grouped_pair", align_bytes=64)
        grouped_main = keep.tile([P, 2, BANDS, 4, 8], BF16, name="grouped_main", align_bytes=64)
        x_codes = keep.tile([P, TOKENS], U32, name="x_codes", align_bytes=64)
        x_scales = keep.tile([P, TOKENS], U8, name="x_scales", align_bytes=64)

        def sort_words(copy, t, ts, jp):
            half = slice(ts * (P // 2), (ts + 1) * (P // 2))
            by_column = pixels[t][:, ts, :].bitcast(F32).rearrange(
                "p (py j q u) -> p j u py q", py=PATCH, j=GRID, q=4, u=2
            )
            pair = slice(2 * jp, 2 * jp + 2)
            copy(
                out=sorted_words[t][:, pair, :, half].rearrange("p j u (py q) -> p j u py q", q=4),
                in_=by_column[:, pair],
            )

        def flip(t, jp):
            flipped = psum_flip.tile([P, 2, 2, P], F32, name="flipped")
            for jj in range(2):
                for u in range(2):
                    nc.tensor.transpose(
                        flipped[:, jj, u, :], sorted_words[t][:, 2 * jp + jj, u, :], identity[:]
                    )
            return flipped

        def gather_row_pair(il, jp, flipped):
            rp = BAND_GRID_ROWS * il + jp
            if rp == 0:
                target = grouped_pair[:].bitcast(F32)
            else:
                target = grouped_main[:].bitcast(F32)[:, (rp - 1) // 4, :, (rp - 1) % 4, :]
            nc.scalar.copy(
                out=target.rearrange("p q (jj u) -> p q jj u", u=2),
                in_=flipped[:, :, :, il % 2 : P : 2].rearrange("p jj u q -> p q jj u"),
            )

        token_tiles = [(0, out_bands[:, 0:2, :])]
        for y in range(2):
            for batch in range(BATCH):
                bands = slice(BATCH_BANDS * batch, BATCH_BANDS * (batch + 1))
                token_tiles.append((1 + y, out_bands[bands, main_rows(y), :]))

        def quantise(first_tile, grouped):
            tokens = slice(P * first_tile, P * first_tile + grouped.shape[1] // 4)
            nc.vector.quantize_mx(
                out=x_codes[:, tokens].bitcast(FP8X4), scales=x_scales[:, tokens], in_=grouped
            )

        def start(tile_index):
            tokens = slice(P * tile_index, P * (tile_index + 1))
            sums = []
            for h in range(2):
                acc = psum_acc.tile([P, N_HALF], F32, name="acc")
                nc.tensor.matmul_mx(
                    out=acc[:],
                    lhsT=x_codes[:, tokens].bitcast(FP8X4),
                    lhsT_scale=x_scales[:, tokens],
                    rhs=w_codes[:, 4 * N_HALF * h : 4 * N_HALF * (h + 1)].bitcast(FP8X4),
                    rhs_scale=w_scales[:, half_cols(h)],
                    start=True,
                    stop=True,
                )
                sums.append(acc)
            return sums

        side_tiles = (3, 4, 5, 6)
        late_stores = []

        def side_half(tile_index, sums, result):
            cols = half_cols(1)
            kind = token_tiles[tile_index][0]
            nc.scalar.copy(out=result[:, cols], in_=sums[1][:])
            nc.gpsimd.tensor_tensor(
                out=result[:, cols], in0=result[:, cols], in1=addend[:, kind, cols], op=ADD
            )
            late_stores.append((token_tiles[tile_index][1][:, :, cols], result[:, cols]))
            if len(late_stores) > 1:
                entry = late_stores[0]
                late_stores.remove(entry)
                nc.scalar.dma_start(out=entry[0], in_=entry[1])

        def finish(tile_index, h, sums, result):
            kind = token_tiles[tile_index][0]
            rows = token_tiles[tile_index][1]
            cols = half_cols(h)
            nc.vector.tensor_tensor(
                out=result[:, cols], in0=sums[h][:], in1=addend[:, kind, cols], op=ADD
            )
            nc.sync.dma_start(out=rows[:, :, cols], in_=result[:, cols])

        def first_addend(h):
            cols = half_cols(h)
            nc.vector.tensor_tensor(
                out=addend[:, 1, cols], in0=bias_bank[:, cols], in1=pos_bf[:, 0, cols], op=ADD
            )

        for ts in range(TUBE):
            for jp in range(GRID // 2):
                sort_words(nc.vector.tensor_copy, 0, ts, jp)
        flipped = [flip(0, jp) for jp in range(GRID // 2)]
        first_addend(0)
        gather_row_pair(0, 0, flipped[0])
        quantise(0, grouped_pair[:].rearrange("p q v -> p (q v)"))
        first_addend(1)
        sums = start(0)
        for il, jp in ((1, 0), (0, 1), (1, 1), (0, 2)):
            gather_row_pair(il, jp, flipped[jp])
        result = results.tile([P, EMBED], F32, name="result")
        finish(0, 0, sums, result)
        quantise(1, grouped_main[:, 0].rearrange("p q a v -> p (q a v)"))
        nc.scalar.copy(out=bias_all[:], in_=bias_bank[:])
        gather_row_pair(1, 2, flipped[2])
        for h in range(2):
            nc.gpsimd.tensor_tensor(
                out=addend[:, 2, half_cols(h)], in0=pos_bf[:, 1, half_cols(h)],
                in1=bias_all[:, half_cols(h)], op=ADD,
            )
        for jp in range(GRID // 2):
            for ts in range(TUBE):
                sort_words(nc.scalar.copy, 1, ts, jp)
        next_sums = start(1)
        finish(0, 1, sums, result)
        sums = next_sums
        late_flips = {1: (0,), 2: (1, 2)}
        for tile_index in range(1, len(token_tiles)):
            next_sums = None
            result = results.tile([P, EMBED], F32, name="result")
            if tile_index == BATCH:
                finish(tile_index, 0, sums, result)
                quantise(BATCH + 1, grouped_main[:, 1].rearrange("p q a v -> p (q a v)"))
            if tile_index + 1 < len(token_tiles):
                next_sums = start(tile_index + 1)
            if tile_index in side_tiles:
                side_half(tile_index, sums, result)
            for jp in late_flips.get(tile_index, ()):
                gather_row_pair(2, jp, flip(1, jp))
            for h in range(2):
                if (tile_index, h) != (BATCH, 0) and not (h == 1 and tile_index in side_tiles):
                    finish(tile_index, h, sums, result)
            sums = next_sums
        for target, source in late_stores:
            nc.scalar.dma_start(out=target, in_=source)
